import numpy as np
import ml_dtypes


BF16 = ml_dtypes.bfloat16


def bf(x):
    return np.asarray(x, np.float32).astype(BF16)


def f64(x):
    return np.asarray(x).astype(np.float64)


E2M1 = np.array([0.0, 0.5, 1.0, 1.5, 2.0, 3.0, 4.0, 6.0, -0.0, -0.5, -1.0, -1.5, -2.0, -3.0, -4.0, -6.0])


def pack_weight(w, fmt):
    k, n = w.shape
    w = f64(bf(w)).reshape(k // 32, 32, n)
    amax = np.abs(w).max(1)
    if fmt == "e4m3":
        byte = np.frexp(amax)[1] - 1 + 127 - 7
    else:
        mant, ex = np.frexp(amax / 6.0)
        byte = np.where(mant > 0.5, ex, ex - 1) + 127
    byte = np.clip(np.where(amax > 0, byte, 1), 1, 254)
    scaled = (w * np.exp2(127.0 - byte)[:, None, :]).reshape(k, n).astype(np.float32)
    by_word = np.ascontiguousarray(scaled.reshape(k // 512, 128, 4, n).transpose(0, 1, 3, 2))
    if fmt == "e4m3":
        words = by_word.astype(ml_dtypes.float8_e4m3fn).view(np.uint8)
    else:
        c = by_word.astype(ml_dtypes.float4_e2m1fn).view(np.uint8) & 0xF
        words = c[..., 0::2] | (c[..., 1::2] << 4)
    return np.ascontiguousarray(words), np.ascontiguousarray(byte.astype(np.uint8).reshape(k // 512, 16, n))


def unpack_weight(words, scales, fmt):
    g, p, n, _ = words.shape
    if fmt == "e4m3":
        vals = np.ascontiguousarray(words).view(ml_dtypes.float8_e4m3fn).astype(np.float64)
    else:
        nib = np.empty((g, p, n, 4), np.uint8)
        nib[..., 0::2] = words & 0xF
        nib[..., 1::2] = words >> 4
        vals = E2M1[nib]
    vals = vals * np.repeat(np.exp2(scales.astype(np.float64) - 127.0), 8, axis=1)[..., None]
    return vals.transpose(0, 1, 3, 2).reshape(g * 512, n)

def pack4(w):
    words, scales = pack_weight(w, "e2m1")
    return words.reshape(words.shape[0], 128, -1), scales


def unpack4(words, scales):
    return unpack_weight(words.reshape(words.shape[0], 128, -1, 2), scales, "e2m1")


def kspread(k):
    return np.exp2(np.repeat(np.random.randint(-6, 7, k // 32), 32).astype(np.float64))


S, D, N_HEADS, N_KV_HEADS, HEAD_DIM = 1024, 1024, 16, 4, 128
Q_DIM = N_HEADS * HEAD_DIM
KV_DIM = N_KV_HEADS * HEAD_DIM
ROPE_THETA = 500000.0


def apply_rope(t, cos, sin):
    te = t[:, :, ::2]
    to = t[:, :, 1::2]
    c = cos[:, None, :]
    s = sin[:, None, :]
    te_rot = te * c - to * s
    to_rot = te * s + to * c
    return np.stack([te_rot, to_rot], axis=-1).reshape(t.shape)


def setup_inputs():
    s = kspread(D)
    inv_freq = 1.0 / ROPE_THETA ** (np.arange(0, HEAD_DIM, 2) / HEAD_DIM)
    angles = np.arange(S)[:, None] * inv_freq[None, :]
    x = np.random.standard_normal((S, D)) * s
    x_words, x_scales = pack4(np.ascontiguousarray(x.reshape(S, D).T))
    freqs_cos = bf(np.cos(angles))
    freqs_sin = bf(np.sin(angles))
    wqkv = np.random.standard_normal((Q_DIM + 2 * KV_DIM, D)) / np.sqrt(D) / s[None, :]
    words, scales = pack4(np.ascontiguousarray(wqkv.T))
    return {"x_words": x_words,
            "x_scales": x_scales,
            "freqs_cos": freqs_cos,
            "freqs_sin": freqs_sin,
            "wqkv_words": words,
            "wqkv_scales": scales}


def reference(x_words, x_scales, freqs_cos, freqs_sin, wqkv_words, wqkv_scales):
    qkv = unpack4(x_words, x_scales).T @ unpack4(wqkv_words, wqkv_scales)
    q = qkv[:, :Q_DIM].reshape(S, N_HEADS, HEAD_DIM)
    k = qkv[:, Q_DIM:Q_DIM + KV_DIM].reshape(S, N_KV_HEADS, HEAD_DIM)
    v = qkv[:, Q_DIM + KV_DIM:].reshape(S, N_KV_HEADS, HEAD_DIM)
    cos, sin = f64(freqs_cos), f64(freqs_sin)
    return apply_rope(q, cos, sin), apply_rope(k, cos, sin), v

@@ -1,0 +1,140 @@
+from contextlib import ExitStack
+
+import concourse.mybir as mybir
+
+F32 = mybir.dt.float32
+BF16 = mybir.dt.bfloat16
+U8 = mybir.dt.uint8
+I32 = mybir.dt.int32
+FP4X4 = mybir.dt.float4_e2m1fn_x4
+MULT = mybir.AluOpType.mult
+ADD = mybir.AluOpType.add
+COPY = mybir.ActivationFunctionType.Copy
+
+S = 1024
+D = 1024
+NQKV = 3072
+P = 128
+PASSES = D // 512
+BANK = 512
+TILES = S // P
+HALF = 64
+
+FLOPS = 2 * S * D * NQKV
+
+
+def tile_mha_pa_kernel(
+    tc, x_words, x_scales, freqs_cos, freqs_sin, wqkv_words, wqkv_scales, out_0, out_1, out_2
+):
+    nc = tc.nc
+    q_out = out_0.rearrange("s h d -> s (h d)")
+    k_out = out_1.rearrange("s h d -> s (h d)")
+    v_out = out_2.rearrange("s h d -> s (h d)")
+
+    with ExitStack() as ctx:
+        keep = ctx.enter_context(tc.tile_pool(name="keep", bufs=1))
+        work = ctx.enter_context(tc.tile_pool(name="work", bufs=3))
+        psum = ctx.enter_context(tc.psum_pool(name="psum", bufs=8))
+
+        xw = keep.tile([P, PASSES, 2 * S], U8, align_bytes=64)
+        xs = keep.tile([P, PASSES, S], U8, align_bytes=64)
+        ww = keep.tile([P, PASSES, 2 * NQKV], U8, align_bytes=64)
+        ws = keep.tile([P, PASSES, NQKV], U8, align_bytes=64)
+        cosb = keep.tile([P, TILES, HALF], BF16)
+        sinb = keep.tile([P, TILES, HALF], BF16)
+        sign = keep.tile([P, TILES * HALF, 2], F32)
+        cos2 = keep.tile([P, TILES, 2 * HALF], F32)
+        sin2 = keep.tile([P, TILES, 2 * HALF], F32)
+        warm = keep.tile([P, 2], F32)
+
+        nc.vector.memset(xs[:].bitcast(I32), 0)
+        nc.vector.memset(ws[:, :, 0:1024].bitcast(I32), 0)
+        nc.vector.memset(ws[:, :, 1024:NQKV].bitcast(I32), 0)
+        nc.gpsimd.memset(warm[:], 0.0)
+        nc.gpsimd.memset(sign[:, :, 0:1], -1.0)
+        nc.gpsimd.memset(sign[:, :, 1:2], 1.0)
+        nc.scalar.activation(out=warm[:, 1:2], in_=warm[:, 0:1], func=COPY)
+
+        nc.gpsimd.dma_start(out=cosb[:], in_=freqs_cos.rearrange("(t p) i -> p t i", p=P))
+        nc.gpsimd.dma_start(out=sinb[:], in_=freqs_sin.rearrange("(t p) i -> p t i", p=P))
+
+        xw_src = x_words.rearrange("g p n -> p g n")
+        ww_src = wqkv_words.rearrange("g p n -> p g n")
+
+        def load_w_codes(c0, c1):
+            nc.sync.dma_start(
+                out=ww[:, :, 2 * c0 : 2 * c1].bitcast(I32), in_=ww_src[:, :, 2 * c0 : 2 * c1].bitcast(I32)
+            )
+
+        def load_scales(plane, src, c0, c1):
+            for quad in range(4):
+                nc.sync.dma_start(
+                    out=plane[32 * quad : 32 * quad + 4, :, c0:c1].bitcast(I32),
+                    in_=src[:, 4 * quad : 4 * quad + 4, c0:c1].rearrange("g r n -> r g n").bitcast(I32),
+                )
+
+        nc.sync.dma_start(out=xw[:, :, 0:512].bitcast(I32), in_=xw_src[:, :, 0:512].bitcast(I32))
+        load_w_codes(0, 1024)
+        load_scales(xs, x_scales, 0, S)
+        load_scales(ws, wqkv_scales, 0, 1024)
+        nc.sync.dma_start(out=xw[:, :, 512 : 2 * S].bitcast(I32), in_=xw_src[:, :, 512 : 2 * S].bitcast(I32))
+        load_w_codes(1024, NQKV)
+        load_scales(ws, wqkv_scales, 1024, NQKV)
+
+        nc.scalar.copy(
+            out=cos2[:].rearrange("p t (i e) -> p (t i) e", e=2),
+            in_=cosb[:].rearrange("p t i -> p (t i)").unsqueeze(2).to_broadcast([P, TILES * HALF, 2]),
+        )
+        nc.vector.tensor_tensor(
+            out=sin2[:].rearrange("p t (i e) -> p (t i) e", e=2),
+            in0=sinb[:].rearrange("p t i -> p (t i)").unsqueeze(2).to_broadcast([P, TILES * HALF, 2]),
+            in1=sign[:],
+            op=MULT,
+        )
+
+        def project(t, b):
+            acc = psum.tile([P, BANK], F32, name="acc")
+            for g in range(PASSES):
+                nc.tensor.matmul_mx(
+                    out=acc[:],
+                    lhsT=xw[:, g, 2 * P * t : 2 * P * (t + 1)].bitcast(FP4X4),
+                    lhsT_scale=xs[:, g, P * t : P * (t + 1)],
+                    rhs=ww[:, g, 2 * BANK * b : 2 * BANK * (b + 1)].bitcast(FP4X4),
+                    rhs_scale=ws[:, g, BANK * b : BANK * (b + 1)],
+                    start=(g == 0),
+                    stop=(g == PASSES - 1),
+                )
+            return acc
+
+        def products(t, acc, t1, t2):
+            heads = BANK // P
+            nc.vector.tensor_tensor(
+                out=t1.rearrange("p (h d) -> p h d", h=heads),
+                in0=acc[:].rearrange("p (h d) -> p h d", h=heads),
+                in1=cos2[:, t, :].unsqueeze(1).to_broadcast([P, heads, P]),
+                op=MULT,
+            )
+            nc.vector.tensor_tensor(
+                out=t2.rearrange("p (h i e) -> p h i e", h=heads, e=2),
+                in0=acc[:].rearrange("p (h i e) -> p h i e", h=heads, e=2)[:, :, :, ::-1],
+                in1=sin2[:, t, :].rearrange("p (i e) -> p i e", e=2).unsqueeze(1).to_broadcast([P, heads, HALF, 2]),
+                op=MULT,
+            )
+
+        for t in range(TILES):
+            rows = slice(P * t, P * (t + 1))
+            for dst, banks in ((q_out[rows, 0:1024], (0, 1)), (q_out[rows, 1024:2048], (2, 3)), (k_out[rows, :], (4,))):
+                width = BANK * len(banks)
+                t1 = work.tile([P, width], F32, name="t1_%d" % len(banks))
+                t2 = work.tile([P, width], F32, name="t2_%d" % len(banks))
+                ro = work.tile([P, width], F32, name="ro_%d" % len(banks))
+                for j, b in enumerate(banks):
+                    acc = project(t, b)
+                    products(t, acc, t1[:, BANK * j : BANK * (j + 1)], t2[:, BANK * j : BANK * (j + 1)])
+                adder = nc.vector if t == TILES - 1 else nc.gpsimd
+                adder.tensor_tensor(out=ro[:], in0=t1[:], in1=t2[:], op=ADD)
+                nc.sync.dma_start(out=dst, in_=ro[:])
+            acc = project(t, 5)
+            vt = work.tile([P, BANK], F32, name="vt")
+            nc.scalar.copy(out=vt[:], in_=acc[:])
+            nc.sync.dma_start(out=v_out[rows, :], in_=vt[:])

@@ -13,14 +13,21 @@ COPY = mybir.ActivationFunctionType.Copy
 
 S = 1024
 D = 1024
+NQ = 2048
 NQKV = 3072
 P = 128
 PASSES = D // 512
 BANK = 512
 TILES = S // P
 HALF = 64
+QH = 16
+KH = 4
+IL = 16
 
 FLOPS = 2 * S * D * NQKV
+
+SCALAR_BANKS = [4,4,4,4,4,4,4,2]
+GP_HEADS = [8,8,8,8,8,8,8,0]
 
 
 def tile_mha_pa_kernel(
@@ -40,23 +47,30 @@ def tile_mha_pa_kernel(
         xs = keep.tile([P, PASSES, S], U8, align_bytes=64)
         ww = keep.tile([P, PASSES, 2 * NQKV], U8, align_bytes=64)
         ws = keep.tile([P, PASSES, NQKV], U8, align_bytes=64)
+        wq = keep.tile([P, PASSES, 2 * NQ], U8, align_bytes=64)
+        wqs = keep.tile([P, PASSES, NQ], U8, align_bytes=64)
         cosb = keep.tile([P, TILES, HALF], BF16)
         sinb = keep.tile([P, TILES, HALF], BF16)
-        sign = keep.tile([P, TILES * HALF, 2], F32)
-        cos2 = keep.tile([P, TILES, 2 * HALF], F32)
-        sin2 = keep.tile([P, TILES, 2 * HALF], F32)
+        sign = keep.tile([P, 2], F32)
+        cosf = keep.tile([P, TILES, HALF], F32)
+        sin2 = keep.tile([P, TILES, HALF, 2], F32)
         warm = keep.tile([P, 2], F32)
 
-        nc.vector.memset(xs[:].bitcast(I32), 0)
-        nc.vector.memset(ws[:, :, 0:1024].bitcast(I32), 0)
-        nc.vector.memset(ws[:, :, 1024:NQKV].bitcast(I32), 0)
-        nc.gpsimd.memset(warm[:], 0.0)
-        nc.gpsimd.memset(sign[:, :, 0:1], -1.0)
-        nc.gpsimd.memset(sign[:, :, 1:2], 1.0)
-        nc.scalar.activation(out=warm[:, 1:2], in_=warm[:, 0:1], func=COPY)
+        ctx.enter_context(tc.manual_schedule())
 
-        nc.gpsimd.dma_start(out=cosb[:], in_=freqs_cos.rearrange("(t p) i -> p t i", p=P))
-        nc.gpsimd.dma_start(out=sinb[:], in_=freqs_sin.rearrange("(t p) i -> p t i", p=P))
+        nc.vector.memset(ws[:, :, 0:NQ].bitcast(I32), 0)
+        nc.vector.memset(xs[:].bitcast(I32), 0)
+        nc.vector.memset(ws[:, :, NQ:NQKV].bitcast(I32), 0)
+        nc.vector.memset(sign[:, 0:1], -1.0)
+        nc.vector.memset(sign[:, 1:2], 1.0)
+        nc.vector.memset(warm[:], 0.0)
+        cos_src = freqs_cos.rearrange("(t p) i -> p t i", p=P)
+        sin_src = freqs_sin.rearrange("(t p) i -> p t i", p=P)
+        nc.gpsimd.dma_start(out=sinb[:, 0:1, :], in_=sin_src[:, 0:1, :])
+        nc.gpsimd.dma_start(out=cosb[:, 0:1, :], in_=cos_src[:, 0:1, :])
+        nc.gpsimd.dma_start(out=sinb[:, 1:TILES, :], in_=sin_src[:, 1:TILES, :])
+        nc.gpsimd.dma_start(out=cosb[:, 1:TILES, :], in_=cos_src[:, 1:TILES, :])
+        nc.scalar.activation(out=warm[:, 1:2], in_=warm[:, 0:1], func=COPY)
 
         xw_src = x_words.rearrange("g p n -> p g n")
         ww_src = wqkv_words.rearrange("g p n -> p g n")
@@ -66,6 +80,11 @@ def tile_mha_pa_kernel(
                 out=ww[:, :, 2 * c0 : 2 * c1].bitcast(I32), in_=ww_src[:, :, 2 * c0 : 2 * c1].bitcast(I32)
             )
 
+        def load_x_codes(c0, c1):
+            nc.sync.dma_start(
+                out=xw[:, :, 2 * c0 : 2 * c1].bitcast(I32), in_=xw_src[:, :, 2 * c0 : 2 * c1].bitcast(I32)
+            )
+
         def load_scales(plane, src, c0, c1):
             for quad in range(4):
                 nc.sync.dma_start(
@@ -73,68 +92,136 @@ def tile_mha_pa_kernel(
                     in_=src[:, 4 * quad : 4 * quad + 4, c0:c1].rearrange("g r n -> r g n").bitcast(I32),
                 )
 
-        nc.sync.dma_start(out=xw[:, :, 0:512].bitcast(I32), in_=xw_src[:, :, 0:512].bitcast(I32))
-        load_w_codes(0, 1024)
+        load_w_codes(0, NQ)
+        load_x_codes(0, 2 * P)
+        load_scales(ws, wqkv_scales, 0, NQ)
         load_scales(xs, x_scales, 0, S)
-        load_scales(ws, wqkv_scales, 0, 1024)
-        nc.sync.dma_start(out=xw[:, :, 512 : 2 * S].bitcast(I32), in_=xw_src[:, :, 512 : 2 * S].bitcast(I32))
-        load_w_codes(1024, NQKV)
-        load_scales(ws, wqkv_scales, 1024, NQKV)
+        load_w_codes(NQ, NQKV)
+        load_scales(ws, wqkv_scales, NQ, NQKV)
+        load_x_codes(2 * P, S)
 
-        nc.scalar.copy(
-            out=cos2[:].rearrange("p t (i e) -> p (t i) e", e=2),
-            in_=cosb[:].rearrange("p t i -> p (t i)").unsqueeze(2).to_broadcast([P, TILES * HALF, 2]),
-        )
-        nc.vector.tensor_tensor(
-            out=sin2[:].rearrange("p t (i e) -> p (t i) e", e=2),
-            in0=sinb[:].rearrange("p t i -> p (t i)").unsqueeze(2).to_broadcast([P, TILES * HALF, 2]),
-            in1=sign[:],
-            op=MULT,
-        )
+        def build_sin(engine, t0, t1):
+            n = (t1 - t0) * HALF
+            engine.tensor_tensor(
+                out=sin2[:, t0:t1, :, :].rearrange("p t i e -> p (t i) e"),
+                in0=sinb[:, t0:t1, :].rearrange("p t i -> p (t i)").unsqueeze(2).to_broadcast([P, n, 2]),
+                in1=sign[:].unsqueeze(1).to_broadcast([P, n, 2]),
+                op=MULT,
+            )
 
-        def project(t, b):
+        build_sin(nc.vector, 0, 1)
+        nc.scalar.copy(out=cosf[:, 0:1, :], in_=cosb[:, 0:1, :])
+        build_sin(nc.gpsimd, 1, TILES)
+        nc.scalar.copy(out=cosf[:, 1:TILES, :], in_=cosb[:, 1:TILES, :])
+
+        for g in range(PASSES):
+            nc.vector.tensor_copy(
+                out=wqs[:, g, :].bitcast(I32).rearrange("p (b h w) -> p b h w", b=4, h=QH),
+                in_=ws[:, g, 0:NQ].bitcast(I32).rearrange("p (h b w) -> p b h w", h=QH, b=4),
+            )
+        for g in range(PASSES):
+            nc.vector.tensor_copy(
+                out=wq[:, g, :].bitcast(I32).rearrange("p (b h w) -> p b h w", b=4, h=QH),
+                in_=ww[:, g, 0 : 2 * NQ].bitcast(I32).rearrange("p (h b w) -> p b h w", h=QH, b=4),
+            )
+
+        def project(t, codes, planes, b):
             acc = psum.tile([P, BANK], F32, name="acc")
             for g in range(PASSES):
                 nc.tensor.matmul_mx(
                     out=acc[:],
                     lhsT=xw[:, g, 2 * P * t : 2 * P * (t + 1)].bitcast(FP4X4),
                     lhsT_scale=xs[:, g, P * t : P * (t + 1)],
-                    rhs=ww[:, g, 2 * BANK * b : 2 * BANK * (b + 1)].bitcast(FP4X4),
-                    rhs_scale=ws[:, g, BANK * b : BANK * (b + 1)],
+                    rhs=codes[:, g, 2 * BANK * b : 2 * BANK * (b + 1)].bitcast(FP4X4),
+                    rhs_scale=planes[:, g, BANK * b : BANK * (b + 1)],
                     start=(g == 0),
                     stop=(g == PASSES - 1),
                 )
             return acc
 
-        def products(t, acc, t1, t2):
-            heads = BANK // P
+        def cos_scalar(t, b, acc, t1c):
+            view = acc[:].rearrange("p (h l e) -> p h l e", h=QH, l=IL)
+            for l in range(IL):
+                i = IL * b + l
+                nc.scalar.activation(out=t1c[:, i, :, :], in_=view[:, :, l, :], func=COPY, scale=cosf[:, t, i : i + 1])
+
+        def cos_vector(t, b, acc, t1c):
             nc.vector.tensor_tensor(
-                out=t1.rearrange("p (h d) -> p h d", h=heads),
-                in0=acc[:].rearrange("p (h d) -> p h d", h=heads),
-                in1=cos2[:, t, :].unsqueeze(1).to_broadcast([P, heads, P]),
-                op=MULT,
-            )
-            nc.vector.tensor_tensor(
-                out=t2.rearrange("p (h i e) -> p h i e", h=heads, e=2),
-                in0=acc[:].rearrange("p (h i e) -> p h i e", h=heads, e=2)[:, :, :, ::-1],
-                in1=sin2[:, t, :].rearrange("p (i e) -> p i e", e=2).unsqueeze(1).to_broadcast([P, heads, HALF, 2]),
+                out=t1c[:, IL * b : IL * (b + 1), :, :],
+                in0=acc[:].rearrange("p (h l e) -> p l h e", h=QH, l=IL),
+                in1=cosf[:, t, IL * b : IL * (b + 1)].unsqueeze(2).unsqueeze(3).to_broadcast([P, IL, QH, 2]),
                 op=MULT,
             )
 
+        def sin_vector(t, b, acc, t2q):
+            nc.vector.tensor_tensor(
+                out=t2q[:, :, IL * b : IL * (b + 1), :],
+                in0=acc[:].rearrange("p (h l e) -> p h l e", h=QH, l=IL)[:, :, :, ::-1],
+                in1=sin2[:, t, IL * b : IL * (b + 1), :].unsqueeze(1).to_broadcast([P, QH, IL, 2]),
+                op=MULT,
+            )
+
+        def products_k(t, acc, t1k, t2k):
+            nc.vector.tensor_tensor(
+                out=t1k[:],
+                in0=acc[:].rearrange("p (h i e) -> p h i e", h=KH, e=2),
+                in1=cosf[:, t, :].unsqueeze(1).unsqueeze(3).to_broadcast([P, KH, HALF, 2]),
+                op=MULT,
+            )
+            nc.vector.tensor_tensor(
+                out=t2k[:],
+                in0=acc[:].rearrange("p (h i e) -> p h i e", h=KH, e=2)[:, :, :, ::-1],
+                in1=sin2[:, t, :, :].unsqueeze(1).to_broadcast([P, KH, HALF, 2]),
+                op=MULT,
+            )
+
+        def add_k(t, t1k, t2k):
+            rok = work.tile([P, KH, HALF, 2], F32, name="rok")
+            nc.vector.tensor_tensor(out=rok[:], in0=t1k[:], in1=t2k[:], op=ADD)
+            nc.sync.dma_start(out=k_out[P * t : P * (t + 1), :], in_=rok[:].rearrange("p h i e -> p (h i e)"))
+
+        def add_q(engine, t, t1c, t2q, roq, h0, h1):
+            engine.tensor_tensor(
+                out=roq[:, h0:h1, :, :],
+                in0=t1c[:].rearrange("p i h e -> p h i e")[:, h0:h1, :, :],
+                in1=t2q[:, h0:h1, :, :],
+                op=ADD,
+            )
+            nc.sync.dma_start(
+                out=q_out[P * t : P * (t + 1), P * h0 : P * h1],
+                in_=roq[:, h0:h1, :, :].rearrange("p h i e -> p (h i e)"),
+            )
+
+        before = None
         for t in range(TILES):
-            rows = slice(P * t, P * (t + 1))
-            for dst, banks in ((q_out[rows, 0:1024], (0, 1)), (q_out[rows, 1024:2048], (2, 3)), (k_out[rows, :], (4,))):
-                width = BANK * len(banks)
-                t1 = work.tile([P, width], F32, name="t1_%d" % len(banks))
-                t2 = work.tile([P, width], F32, name="t2_%d" % len(banks))
-                ro = work.tile([P, width], F32, name="ro_%d" % len(banks))
-                for j, b in enumerate(banks):
-                    acc = project(t, b)
-                    products(t, acc, t1[:, BANK * j : BANK * (j + 1)], t2[:, BANK * j : BANK * (j + 1)])
-                adder = nc.vector if t == TILES - 1 else nc.gpsimd
-                adder.tensor_tensor(out=ro[:], in0=t1[:], in1=t2[:], op=ADD)
-                nc.sync.dma_start(out=dst, in_=ro[:])
-            acc = project(t, 5)
+            acc_q = [project(t, wq, wqs, b) for b in range(4)]
+            acc_k = project(t, ww, ws, 4)
+            acc_v = project(t, ww, ws, 5)
+
+            t1c = work.tile([P, HALF, QH, 2], F32, name="t1c")
+            t2q = work.tile([P, QH, HALF, 2], F32, name="t2q")
+            roq = work.tile([P, QH, HALF, 2], F32, name="roq")
+            t1k = work.tile([P, KH, HALF, 2], F32, name="t1k")
+            t2k = work.tile([P, KH, HALF, 2], F32, name="t2k")
             vt = work.tile([P, BANK], F32, name="vt")
-            nc.scalar.copy(out=vt[:], in_=acc[:])
-            nc.sync.dma_start(out=v_out[rows, :], in_=vt[:])
+            for b in range(4):
+                if b < SCALAR_BANKS[t]:
+                    cos_scalar(t, b, acc_q[b], t1c)
+                else:
+                    cos_vector(t, b, acc_q[b], t1c)
+            nc.scalar.copy(out=vt[:], in_=acc_v[:])
+            for b in range(3):
+                sin_vector(t, b, acc_q[b], t2q)
+            products_k(t, acc_k, t1k, t2k)
+            if before is not None:
+                bt, b1, b2, bo = before
+                add_q(nc.vector, bt, b1, b2, bo, GP_HEADS[bt], QH)
+            add_k(t, t1k, t2k)
+            sin_vector(t, 3, acc_q[3], t2q)
+            nc.sync.dma_start(out=v_out[P * t : P * (t + 1), :], in_=vt[:])
+            if GP_HEADS[t] > 0:
+                add_q(nc.gpsimd, t, t1c, t2q, roq, 0, GP_HEADS[t])
+            before = (t, t1c, t2q, roq)
+        bt, b1, b2, bo = before
+        for h in range(GP_HEADS[bt], QH, 4):
+            add_q(nc.vector, bt, b1, b2, bo, h, h + 4)

@@ -26,8 +26,7 @@ IL = 16
 
 FLOPS = 2 * S * D * NQKV
 
-SCALAR_BANKS = [4,4,4,4,4,4,4,2]
-GP_HEADS = [8,8,8,8,8,8,8,0]
+GP_HEADS = [3, 3, 3, 3, 3, 3, 3, 0]
 
 
 def tile_mha_pa_kernel(
@@ -112,7 +111,6 @@ def tile_mha_pa_kernel(
         build_sin(nc.vector, 0, 1)
         nc.scalar.copy(out=cosf[:, 0:1, :], in_=cosb[:, 0:1, :])
         build_sin(nc.gpsimd, 1, TILES)
-        nc.scalar.copy(out=cosf[:, 1:TILES, :], in_=cosb[:, 1:TILES, :])
 
         for g in range(PASSES):
             nc.vector.tensor_copy(
@@ -145,14 +143,6 @@ def tile_mha_pa_kernel(
                 i = IL * b + l
                 nc.scalar.activation(out=t1c[:, i, :, :], in_=view[:, :, l, :], func=COPY, scale=cosf[:, t, i : i + 1])
 
-        def cos_vector(t, b, acc, t1c):
-            nc.vector.tensor_tensor(
-                out=t1c[:, IL * b : IL * (b + 1), :, :],
-                in0=acc[:].rearrange("p (h l e) -> p l h e", h=QH, l=IL),
-                in1=cosf[:, t, IL * b : IL * (b + 1)].unsqueeze(2).unsqueeze(3).to_broadcast([P, IL, QH, 2]),
-                op=MULT,
-            )
-
         def sin_vector(t, b, acc, t2q):
             nc.vector.tensor_tensor(
                 out=t2q[:, :, IL * b : IL * (b + 1), :],
@@ -161,13 +151,15 @@ def tile_mha_pa_kernel(
                 op=MULT,
             )
 
-        def products_k(t, acc, t1k, t2k):
+        def cos_k(t, acc, t1k):
             nc.vector.tensor_tensor(
                 out=t1k[:],
                 in0=acc[:].rearrange("p (h i e) -> p h i e", h=KH, e=2),
                 in1=cosf[:, t, :].unsqueeze(1).unsqueeze(3).to_broadcast([P, KH, HALF, 2]),
                 op=MULT,
             )
+
+        def sin_k(t, acc, t2k):
             nc.vector.tensor_tensor(
                 out=t2k[:],
                 in0=acc[:].rearrange("p (h i e) -> p h i e", h=KH, e=2)[:, :, :, ::-1],
@@ -175,9 +167,9 @@ def tile_mha_pa_kernel(
                 op=MULT,
             )
 
-        def add_k(t, t1k, t2k):
+        def add_k(engine, t, t1k, t2k):
             rok = work.tile([P, KH, HALF, 2], F32, name="rok")
-            nc.vector.tensor_tensor(out=rok[:], in0=t1k[:], in1=t2k[:], op=ADD)
+            engine.tensor_tensor(out=rok[:], in0=t1k[:], in1=t2k[:], op=ADD)
             nc.sync.dma_start(out=k_out[P * t : P * (t + 1), :], in_=rok[:].rearrange("p h i e -> p (h i e)"))
 
         def add_q(engine, t, t1c, t2q, roq, h0, h1):
@@ -194,6 +186,7 @@ def tile_mha_pa_kernel(
 
         before = None
         for t in range(TILES):
+            last = t == TILES - 1
             acc_q = [project(t, wq, wqs, b) for b in range(4)]
             acc_k = project(t, ww, ws, 4)
             acc_v = project(t, ww, ws, 5)
@@ -205,22 +198,23 @@ def tile_mha_pa_kernel(
             t2k = work.tile([P, KH, HALF, 2], F32, name="t2k")
             vt = work.tile([P, BANK], F32, name="vt")
             for b in range(4):
-                if b < SCALAR_BANKS[t]:
-                    cos_scalar(t, b, acc_q[b], t1c)
-                else:
-                    cos_vector(t, b, acc_q[b], t1c)
-            nc.scalar.copy(out=vt[:], in_=acc_v[:])
-            for b in range(3):
                 sin_vector(t, b, acc_q[b], t2q)
-            products_k(t, acc_k, t1k, t2k)
+                cos_scalar(t, b, acc_q[b], t1c)
+            nc.scalar.copy(out=vt[:], in_=acc_v[:])
+            if t == 0:
+                nc.scalar.copy(out=cosf[:, 1:TILES, :], in_=cosb[:, 1:TILES, :])
+            cos_k(t, acc_k, t1k)
+            if last:
+                sin_k(t, acc_k, t2k)
+                add_k(nc.vector, t, t1k, t2k)
             if before is not None:
                 bt, b1, b2, bo = before
                 add_q(nc.vector, bt, b1, b2, bo, GP_HEADS[bt], QH)
-            add_k(t, t1k, t2k)
-            sin_vector(t, 3, acc_q[3], t2q)
-            nc.sync.dma_start(out=v_out[P * t : P * (t + 1), :], in_=vt[:])
-            if GP_HEADS[t] > 0:
+            if not last:
+                sin_k(t, acc_k, t2k)
+                add_k(nc.gpsimd, t, t1k, t2k)
                 add_q(nc.gpsimd, t, t1c, t2q, roq, 0, GP_HEADS[t])
+            nc.sync.dma_start(out=v_out[P * t : P * (t + 1), :], in_=vt[:])
             before = (t, t1c, t2q, roq)
         bt, b1, b2, bo = before
         for h in range(GP_HEADS[bt], QH, 4):

@@ -26,7 +26,7 @@ IL = 16
 
 FLOPS = 2 * S * D * NQKV
 
-GP_HEADS = [3, 3, 3, 3, 3, 3, 3, 0]
+GP_HEADS = [5, 5, 5, 5, 5, 5, 5, 0]
 
 
 def tile_mha_pa_kernel(
@@ -217,5 +217,5 @@ def tile_mha_pa_kernel(
             nc.sync.dma_start(out=v_out[P * t : P * (t + 1), :], in_=vt[:])
             before = (t, t1c, t2q, roq)
         bt, b1, b2, bo = before
-        for h in range(GP_HEADS[bt], QH, 4):
-            add_q(nc.vector, bt, b1, b2, bo, h, h + 4)
+        for h0, h1 in ((0, 6), (6, 11), (11, 14), (14, QH)):
+            add_q(nc.vector, bt, b1, b2, bo, h0, h1)

@@ -23,10 +23,9 @@ HALF = 64
 QH = 16
 KH = 4
 IL = 16
+SPAIRS = 48
 
 FLOPS = 2 * S * D * NQKV
-
-GP_HEADS = [5, 5, 5, 5, 5, 5, 5, 0]
 
 
 def tile_mha_pa_kernel(
@@ -172,26 +171,49 @@ def tile_mha_pa_kernel(
             engine.tensor_tensor(out=rok[:], in0=t1k[:], in1=t2k[:], op=ADD)
             nc.sync.dma_start(out=k_out[P * t : P * (t + 1), :], in_=rok[:].rearrange("p h i e -> p (h i e)"))
 
-        def add_q(engine, t, t1c, t2q, roq, h0, h1):
+        def cos_q3(t, acc, t1v):
+            nc.vector.tensor_tensor(
+                out=t1v[:],
+                in0=acc[:].rearrange("p (h l e) -> p h l e", h=QH, l=IL),
+                in1=cosf[:, t, SPAIRS:HALF].unsqueeze(1).unsqueeze(3).to_broadcast([P, QH, IL, 2]),
+                op=MULT,
+            )
+
+        def add_bank(engine, b, t1c, t2q, roq):
             engine.tensor_tensor(
-                out=roq[:, h0:h1, :, :],
-                in0=t1c[:].rearrange("p i h e -> p h i e")[:, h0:h1, :, :],
-                in1=t2q[:, h0:h1, :, :],
+                out=roq[:, :, IL * b : IL * (b + 1), :],
+                in0=t1c[:, IL * b : IL * (b + 1), :, :].rearrange("p i h e -> p h i e"),
+                in1=t2q[:, :, IL * b : IL * (b + 1), :],
                 op=ADD,
             )
+
+        def add_q3(t1v, t2q, roq):
+            nc.vector.tensor_tensor(
+                out=roq[:, :, SPAIRS:HALF, :], in0=t1v[:], in1=t2q[:, :, SPAIRS:HALF, :], op=ADD
+            )
+
+        def add_heads(t1c, t2q, roq, h0, h1):
+            nc.vector.tensor_tensor(
+                out=roq[:, h0:h1, 0:SPAIRS, :],
+                in0=t1c[:].rearrange("p i h e -> p h i e")[:, h0:h1, :, :],
+                in1=t2q[:, h0:h1, 0:SPAIRS, :],
+                op=ADD,
+            )
+
+        def store_q(t, roq, h0, h1):
             nc.sync.dma_start(
                 out=q_out[P * t : P * (t + 1), P * h0 : P * h1],
                 in_=roq[:, h0:h1, :, :].rearrange("p h i e -> p (h i e)"),
             )
 
-        before = None
         for t in range(TILES):
             last = t == TILES - 1
             acc_q = [project(t, wq, wqs, b) for b in range(4)]
             acc_k = project(t, ww, ws, 4)
             acc_v = project(t, ww, ws, 5)
 
-            t1c = work.tile([P, HALF, QH, 2], F32, name="t1c")
+            t1c = work.tile([P, SPAIRS, QH, 2], F32, name="t1c")
+            t1v = work.tile([P, QH, IL, 2], F32, name="t1v")
             t2q = work.tile([P, QH, HALF, 2], F32, name="t2q")
             roq = work.tile([P, QH, HALF, 2], F32, name="roq")
             t1k = work.tile([P, KH, HALF, 2], F32, name="t1k")
@@ -199,23 +221,22 @@ def tile_mha_pa_kernel(
             vt = work.tile([P, BANK], F32, name="vt")
             for b in range(4):
                 sin_vector(t, b, acc_q[b], t2q)
-                cos_scalar(t, b, acc_q[b], t1c)
+                if b < 3:
+                    cos_scalar(t, b, acc_q[b], t1c)
             nc.scalar.copy(out=vt[:], in_=acc_v[:])
             if t == 0:
                 nc.scalar.copy(out=cosf[:, 1:TILES, :], in_=cosb[:, 1:TILES, :])
+            cos_q3(t, acc_q[3], t1v)
             cos_k(t, acc_k, t1k)
-            if last:
-                sin_k(t, acc_k, t2k)
-                add_k(nc.vector, t, t1k, t2k)
-            if before is not None:
-                bt, b1, b2, bo = before
-                add_q(nc.vector, bt, b1, b2, bo, GP_HEADS[bt], QH)
-            if not last:
-                sin_k(t, acc_k, t2k)
-                add_k(nc.gpsimd, t, t1k, t2k)
-                add_q(nc.gpsimd, t, t1c, t2q, roq, 0, GP_HEADS[t])
+            sin_k(t, acc_k, t2k)
+            add_q3(t1v, t2q, roq)
+            add_k(nc.vector, t, t1k, t2k)
             nc.sync.dma_start(out=v_out[P * t : P * (t + 1), :], in_=vt[:])
-            before = (t, t1c, t2q, roq)
-        bt, b1, b2, bo = before
-        for h0, h1 in ((0, 6), (6, 11), (11, 14), (14, QH)):
-            add_q(nc.vector, bt, b1, b2, bo, h0, h1)
+            if not last:
+                for b in range(3):
+                    add_bank(nc.gpsimd, b, t1c, t2q, roq)
+                store_q(t, roq, 0, QH)
+            else:
+                for h0, h1 in ((0, 6), (6, 11), (11, 14), (14, QH)):
+                    add_heads(t1c, t2q, roq, h0, h1)
+                    store_q(t, roq, h0, h1)

@@ -24,6 +24,7 @@ QH = 16
 KH = 4
 IL = 16
 SPAIRS = 48
+WARM_UP = 18
 
 FLOPS = 2 * S * D * NQKV
 
@@ -53,15 +54,18 @@ def tile_mha_pa_kernel(
         cosf = keep.tile([P, TILES, HALF], F32)
         sin2 = keep.tile([P, TILES, HALF, 2], F32)
         warm = keep.tile([P, 2], F32)
+        idle = keep.tile([P, BANK], BF16)
 
         ctx.enter_context(tc.manual_schedule())
 
-        nc.vector.memset(ws[:, :, 0:NQ].bitcast(I32), 0)
         nc.vector.memset(xs[:].bitcast(I32), 0)
+        nc.vector.memset(ws[:, :, 0:NQ].bitcast(I32), 0)
         nc.vector.memset(ws[:, :, NQ:NQKV].bitcast(I32), 0)
-        nc.vector.memset(sign[:, 0:1], -1.0)
-        nc.vector.memset(sign[:, 1:2], 1.0)
         nc.vector.memset(warm[:], 0.0)
+        nc.vector.memset(idle[:], 0.0)
+        spin = psum.tile([P, BANK], F32, name="acc")
+        for n in range(WARM_UP):
+            nc.tensor.matmul(out=spin[:], lhsT=idle[:, 0:P], rhs=idle[:], start=True, stop=True)
         cos_src = freqs_cos.rearrange("(t p) i -> p t i", p=P)
         sin_src = freqs_sin.rearrange("(t p) i -> p t i", p=P)
         nc.gpsimd.dma_start(out=sinb[:, 0:1, :], in_=sin_src[:, 0:1, :])
@@ -84,16 +88,16 @@ def tile_mha_pa_kernel(
             )
 
         def load_scales(plane, src, c0, c1):
-            for quad in range(4):
+            for r in range(4):
                 nc.sync.dma_start(
-                    out=plane[32 * quad : 32 * quad + 4, :, c0:c1].bitcast(I32),
-                    in_=src[:, 4 * quad : 4 * quad + 4, c0:c1].rearrange("g r n -> r g n").bitcast(I32),
+                    out=plane[r : P : 32, :, c0:c1].bitcast(I32),
+                    in_=src[:, r : 16 : 4, c0:c1].rearrange("g q n -> q g n").bitcast(I32),
                 )
 
-        load_w_codes(0, NQ)
         load_x_codes(0, 2 * P)
-        load_scales(ws, wqkv_scales, 0, NQ)
         load_scales(xs, x_scales, 0, S)
+        load_w_codes(0, NQ)
+        load_scales(ws, wqkv_scales, 0, NQ)
         load_w_codes(NQ, NQKV)
         load_scales(ws, wqkv_scales, NQ, NQKV)
         load_x_codes(2 * P, S)
@@ -107,20 +111,23 @@ def tile_mha_pa_kernel(
                 op=MULT,
             )
 
-        build_sin(nc.vector, 0, 1)
         nc.scalar.copy(out=cosf[:, 0:1, :], in_=cosb[:, 0:1, :])
-        build_sin(nc.gpsimd, 1, TILES)
 
-        for g in range(PASSES):
-            nc.vector.tensor_copy(
-                out=wqs[:, g, :].bitcast(I32).rearrange("p (b h w) -> p b h w", b=4, h=QH),
-                in_=ws[:, g, 0:NQ].bitcast(I32).rearrange("p (h b w) -> p b h w", h=QH, b=4),
-            )
         for g in range(PASSES):
             nc.vector.tensor_copy(
                 out=wq[:, g, :].bitcast(I32).rearrange("p (b h w) -> p b h w", b=4, h=QH),
                 in_=ww[:, g, 0 : 2 * NQ].bitcast(I32).rearrange("p (h b w) -> p b h w", h=QH, b=4),
             )
+        for g in range(PASSES):
+            nc.vector.tensor_copy(
+                out=wqs[:, g, :].bitcast(I32).rearrange("p (b h w) -> p b h w", b=4, h=QH),
+                in_=ws[:, g, 0:NQ].bitcast(I32).rearrange("p (h b w) -> p b h w", h=QH, b=4),
+            )
+
+        nc.vector.memset(sign[:, 0:1], -1.0)
+        nc.vector.memset(sign[:, 1:2], 1.0)
+        build_sin(nc.vector, 0, 1)
+        build_sin(nc.gpsimd, 1, TILES)
 
         def project(t, codes, planes, b):
             acc = psum.tile([P, BANK], F32, name="acc")

@@ -1,6 +1,7 @@
 from contextlib import ExitStack
 
 import concourse.mybir as mybir
+from concourse.masks import make_identity
 
 F32 = mybir.dt.float32
 BF16 = mybir.dt.bfloat16
@@ -54,6 +55,7 @@ def tile_mha_pa_kernel(
         cosf = keep.tile([P, TILES, HALF], F32)
         sin2 = keep.tile([P, TILES, HALF, 2], F32)
         warm = keep.tile([P, 2], F32)
+        ident = keep.tile([P, P], F32)
         idle = keep.tile([P, BANK], BF16)
 
         ctx.enter_context(tc.manual_schedule())
@@ -73,6 +75,7 @@ def tile_mha_pa_kernel(
         nc.gpsimd.dma_start(out=sinb[:, 1:TILES, :], in_=sin_src[:, 1:TILES, :])
         nc.gpsimd.dma_start(out=cosb[:, 1:TILES, :], in_=cos_src[:, 1:TILES, :])
         nc.scalar.activation(out=warm[:, 1:2], in_=warm[:, 0:1], func=COPY)
+        make_identity(nc, ident[:])
 
         xw_src = x_words.rearrange("g p n -> p g n")
         ww_src = wqkv_words.rearrange("g p n -> p g n")
@@ -213,12 +216,18 @@ def tile_mha_pa_kernel(
                 in_=roq[:, h0:h1, :, :].rearrange("p h i e -> p (h i e)"),
             )
 
+        def project_tile(t):
+            return [project(t, wq, wqs, b) for b in range(4)], project(t, ww, ws, 4), project(t, ww, ws, 5)
+
+        def copy_k(t, acc_r):
+            rok = work.tile([P, BANK], F32, name="rok")
+            nc.scalar.copy(out=rok[:], in_=acc_r[:])
+            nc.sync.dma_start(out=k_out[P * t : P * (t + 1), :], in_=rok[:])
+
+        acc_q, acc_k, acc_v = project_tile(0)
+        waiting = None
         for t in range(TILES):
             last = t == TILES - 1
-            acc_q = [project(t, wq, wqs, b) for b in range(4)]
-            acc_k = project(t, ww, ws, 4)
-            acc_v = project(t, ww, ws, 5)
-
             t1c = work.tile([P, SPAIRS, QH, 2], F32, name="t1c")
             t1v = work.tile([P, QH, IL, 2], F32, name="t1v")
             t2q = work.tile([P, QH, HALF, 2], F32, name="t2q")
@@ -226,18 +235,28 @@ def tile_mha_pa_kernel(
             t1k = work.tile([P, KH, HALF, 2], F32, name="t1k")
             t2k = work.tile([P, KH, HALF, 2], F32, name="t2k")
             vt = work.tile([P, BANK], F32, name="vt")
-            for b in range(4):
+            for b in range(3):
                 sin_vector(t, b, acc_q[b], t2q)
-                if b < 3:
-                    cos_scalar(t, b, acc_q[b], t1c)
+                cos_scalar(t, b, acc_q[b], t1c)
+            if waiting is not None:
+                copy_k(t - 1, waiting)
+                waiting = None
             nc.scalar.copy(out=vt[:], in_=acc_v[:])
             if t == 0:
                 nc.scalar.copy(out=cosf[:, 1:TILES, :], in_=cosb[:, 1:TILES, :])
+            sin_vector(t, 3, acc_q[3], t2q)
             cos_q3(t, acc_q[3], t1v)
             cos_k(t, acc_k, t1k)
             sin_k(t, acc_k, t2k)
+            if not last:
+                acc_q, acc_k, acc_v = project_tile(t + 1)
+            if t % 2 == 0:
+                waiting = psum.tile([P, BANK], F32, name="acc")
+                nc.tensor.matmul(out=waiting[:], lhsT=ident[:], rhs=t1k[:].rearrange("p h i e -> p (h i e)"), start=True, stop=False)
+                nc.tensor.matmul(out=waiting[:], lhsT=ident[:], rhs=t2k[:].rearrange("p h i e -> p (h i e)"), start=False, stop=True)
             add_q3(t1v, t2q, roq)
-            add_k(nc.vector, t, t1k, t2k)
+            if t % 2 == 1:
+                add_k(nc.vector, t, t1k, t2k)
             nc.sync.dma_start(out=v_out[P * t : P * (t + 1), :], in_=vt[:])
             if not last:
                 for b in range(3):

@@ -224,8 +224,15 @@ def tile_mha_pa_kernel(
             nc.scalar.copy(out=rok[:], in_=acc_r[:])
             nc.sync.dma_start(out=k_out[P * t : P * (t + 1), :], in_=rok[:])
 
+        def finish(t, t1v, t2q, roq, t1k, t2k):
+            add_q3(t1v, t2q, roq)
+            if t % 2 == 1:
+                add_k(nc.vector, t, t1k, t2k)
+            store_q(t, roq, 0, QH)
+
         acc_q, acc_k, acc_v = project_tile(0)
         waiting = None
+        owed = None
         for t in range(TILES):
             last = t == TILES - 1
             t1c = work.tile([P, SPAIRS, QH, 2], F32, name="t1c")
@@ -238,6 +245,9 @@ def tile_mha_pa_kernel(
             for b in range(3):
                 sin_vector(t, b, acc_q[b], t2q)
                 cos_scalar(t, b, acc_q[b], t1c)
+                if b == 1 and owed is not None:
+                    finish(*owed)
+                    owed = None
             if waiting is not None:
                 copy_k(t - 1, waiting)
                 waiting = None
@@ -254,15 +264,14 @@ def tile_mha_pa_kernel(
                 waiting = psum.tile([P, BANK], F32, name="acc")
                 nc.tensor.matmul(out=waiting[:], lhsT=ident[:], rhs=t1k[:].rearrange("p h i e -> p (h i e)"), start=True, stop=False)
                 nc.tensor.matmul(out=waiting[:], lhsT=ident[:], rhs=t2k[:].rearrange("p h i e -> p (h i e)"), start=False, stop=True)
-            add_q3(t1v, t2q, roq)
-            if t % 2 == 1:
-                add_k(nc.vector, t, t1k, t2k)
             nc.sync.dma_start(out=v_out[P * t : P * (t + 1), :], in_=vt[:])
             if not last:
                 for b in range(3):
                     add_bank(nc.gpsimd, b, t1c, t2q, roq)
-                store_q(t, roq, 0, QH)
+                owed = (t, t1v, t2q, roq, t1k, t2k)
             else:
+                add_q3(t1v, t2q, roq)
+                add_k(nc.vector, t, t1k, t2k)
                 for h0, h1 in ((0, 6), (6, 11), (11, 14), (14, QH)):
                     add_heads(t1c, t2q, roq, h0, h1)
                     store_q(t, roq, h0, h1)

@@ -197,8 +197,8 @@ def tile_mha_pa_kernel(
                 op=ADD,
             )
 
-        def add_q3(t1v, t2q, roq):
-            nc.vector.tensor_tensor(
+        def add_q3(engine, t1v, t2q, roq):
+            engine.tensor_tensor(
                 out=roq[:, :, SPAIRS:HALF, :], in0=t1v[:], in1=t2q[:, :, SPAIRS:HALF, :], op=ADD
             )
 
@@ -224,8 +224,8 @@ def tile_mha_pa_kernel(
             nc.scalar.copy(out=rok[:], in_=acc_r[:])
             nc.sync.dma_start(out=k_out[P * t : P * (t + 1), :], in_=rok[:])
 
-        def finish(t, t1v, t2q, roq, t1k, t2k):
-            add_q3(t1v, t2q, roq)
+        def finish(t, t1c, t2q, roq, t1k, t2k):
+            add_bank(nc.vector, 2, t1c, t2q, roq)
             if t % 2 == 1:
                 add_k(nc.vector, t, t1k, t2k)
             store_q(t, roq, 0, QH)
@@ -266,11 +266,12 @@ def tile_mha_pa_kernel(
                 nc.tensor.matmul(out=waiting[:], lhsT=ident[:], rhs=t2k[:].rearrange("p h i e -> p (h i e)"), start=False, stop=True)
             nc.sync.dma_start(out=v_out[P * t : P * (t + 1), :], in_=vt[:])
             if not last:
-                for b in range(3):
-                    add_bank(nc.gpsimd, b, t1c, t2q, roq)
-                owed = (t, t1v, t2q, roq, t1k, t2k)
+                add_bank(nc.gpsimd, 0, t1c, t2q, roq)
+                add_bank(nc.gpsimd, 1, t1c, t2q, roq)
+                add_q3(nc.gpsimd, t1v, t2q, roq)
+                owed = (t, t1c, t2q, roq, t1k, t2k)
             else:
-                add_q3(t1v, t2q, roq)
+                add_q3(nc.vector, t1v, t2q, roq)
                 add_k(nc.vector, t, t1k, t2k)
                 for h0, h1 in ((0, 6), (6, 11), (11, 14), (14, QH)):
                     add_heads(t1c, t2q, roq, h0, h1)

from contextlib import ExitStack

import concourse.mybir as mybir
from concourse.masks import make_identity

F32 = mybir.dt.float32
BF16 = mybir.dt.bfloat16
U8 = mybir.dt.uint8
I32 = mybir.dt.int32
FP4X4 = mybir.dt.float4_e2m1fn_x4
MULT = mybir.AluOpType.mult
ADD = mybir.AluOpType.add
COPY = mybir.ActivationFunctionType.Copy

S = 1024
D = 1024
NQ = 2048
NQKV = 3072
P = 128
PASSES = D // 512
BANK = 512
TILES = S // P
HALF = 64
QH = 16
KH = 4
IL = 16
SPAIRS = 48
WARM_UP = 18

FLOPS = 2 * S * D * NQKV


def tile_mha_pa_kernel(
    tc, x_words, x_scales, freqs_cos, freqs_sin, wqkv_words, wqkv_scales, out_0, out_1, out_2
):
    nc = tc.nc
    q_out = out_0.rearrange("s h d -> s (h d)")
    k_out = out_1.rearrange("s h d -> s (h d)")
    v_out = out_2.rearrange("s h d -> s (h d)")

    with ExitStack() as ctx:
        keep = ctx.enter_context(tc.tile_pool(name="keep", bufs=1))
        work = ctx.enter_context(tc.tile_pool(name="work", bufs=3))
        psum = ctx.enter_context(tc.psum_pool(name="psum", bufs=8))

        xw = keep.tile([P, PASSES, 2 * S], U8, align_bytes=64)
        xs = keep.tile([P, PASSES, S], U8, align_bytes=64)
        ww = keep.tile([P, PASSES, 2 * NQKV], U8, align_bytes=64)
        ws = keep.tile([P, PASSES, NQKV], U8, align_bytes=64)
        wq = keep.tile([P, PASSES, 2 * NQ], U8, align_bytes=64)
        wqs = keep.tile([P, PASSES, NQ], U8, align_bytes=64)
        cosb = keep.tile([P, TILES, HALF], BF16)
        sinb = keep.tile([P, TILES, HALF], BF16)
        sign = keep.tile([P, 2], F32)
        cosf = keep.tile([P, TILES, HALF], F32)
        sin2 = keep.tile([P, TILES, HALF, 2], F32)
        warm = keep.tile([P, 2], F32)
        ident = keep.tile([P, P], F32)
        idle = keep.tile([P, BANK], BF16)

        ctx.enter_context(tc.manual_schedule())

        nc.vector.memset(xs[:].bitcast(I32), 0)
        nc.vector.memset(ws[:, :, 0:NQ].bitcast(I32), 0)
        nc.vector.memset(ws[:, :, NQ:NQKV].bitcast(I32), 0)
        nc.vector.memset(warm[:], 0.0)
        nc.vector.memset(idle[:], 0.0)
        spin = psum.tile([P, BANK], F32, name="acc")
        for n in range(WARM_UP):
            nc.tensor.matmul(out=spin[:], lhsT=idle[:, 0:P], rhs=idle[:], start=True, stop=True)
        cos_src = freqs_cos.rearrange("(t p) i -> p t i", p=P)
        sin_src = freqs_sin.rearrange("(t p) i -> p t i", p=P)
        nc.gpsimd.dma_start(out=sinb[:, 0:1, :], in_=sin_src[:, 0:1, :])
        nc.gpsimd.dma_start(out=cosb[:, 0:1, :], in_=cos_src[:, 0:1, :])
        nc.gpsimd.dma_start(out=sinb[:, 1:TILES, :], in_=sin_src[:, 1:TILES, :])
        nc.gpsimd.dma_start(out=cosb[:, 1:TILES, :], in_=cos_src[:, 1:TILES, :])
        nc.scalar.activation(out=warm[:, 1:2], in_=warm[:, 0:1], func=COPY)
        make_identity(nc, ident[:])

        xw_src = x_words.rearrange("g p n -> p g n")
        ww_src = wqkv_words.rearrange("g p n -> p g n")

        def load_w_codes(c0, c1):
            nc.sync.dma_start(
                out=ww[:, :, 2 * c0 : 2 * c1].bitcast(I32), in_=ww_src[:, :, 2 * c0 : 2 * c1].bitcast(I32)
            )

        def load_x_codes(c0, c1):
            nc.sync.dma_start(
                out=xw[:, :, 2 * c0 : 2 * c1].bitcast(I32), in_=xw_src[:, :, 2 * c0 : 2 * c1].bitcast(I32)
            )

        def load_scales(plane, src, c0, c1):
            for r in range(4):
                nc.sync.dma_start(
                    out=plane[r : P : 32, :, c0:c1].bitcast(I32),
                    in_=src[:, r : 16 : 4, c0:c1].rearrange("g q n -> q g n").bitcast(I32),
                )

        load_x_codes(0, 2 * P)
        load_scales(xs, x_scales, 0, S)
        load_w_codes(0, NQ)
        load_scales(ws, wqkv_scales, 0, NQ)
        load_w_codes(NQ, NQKV)
        load_scales(ws, wqkv_scales, NQ, NQKV)
        load_x_codes(2 * P, S)

        def build_sin(engine, t0, t1):
            n = (t1 - t0) * HALF
            engine.tensor_tensor(
                out=sin2[:, t0:t1, :, :].rearrange("p t i e -> p (t i) e"),
                in0=sinb[:, t0:t1, :].rearrange("p t i -> p (t i)").unsqueeze(2).to_broadcast([P, n, 2]),
                in1=sign[:].unsqueeze(1).to_broadcast([P, n, 2]),
                op=MULT,
            )

        nc.scalar.copy(out=cosf[:, 0:1, :], in_=cosb[:, 0:1, :])

        for g in range(PASSES):
            nc.vector.tensor_copy(
                out=wq[:, g, :].bitcast(I32).rearrange("p (b h w) -> p b h w", b=4, h=QH),
                in_=ww[:, g, 0 : 2 * NQ].bitcast(I32).rearrange("p (h b w) -> p b h w", h=QH, b=4),
            )
        for g in range(PASSES):
            nc.vector.tensor_copy(
                out=wqs[:, g, :].bitcast(I32).rearrange("p (b h w) -> p b h w", b=4, h=QH),
                in_=ws[:, g, 0:NQ].bitcast(I32).rearrange("p (h b w) -> p b h w", h=QH, b=4),
            )

        nc.vector.memset(sign[:, 0:1], -1.0)
        nc.vector.memset(sign[:, 1:2], 1.0)
        build_sin(nc.vector, 0, 1)
        build_sin(nc.gpsimd, 1, TILES)

        def project(t, codes, planes, b):
            acc = psum.tile([P, BANK], F32, name="acc")
            for g in range(PASSES):
                nc.tensor.matmul_mx(
                    out=acc[:],
                    lhsT=xw[:, g, 2 * P * t : 2 * P * (t + 1)].bitcast(FP4X4),
                    lhsT_scale=xs[:, g, P * t : P * (t + 1)],
                    rhs=codes[:, g, 2 * BANK * b : 2 * BANK * (b + 1)].bitcast(FP4X4),
                    rhs_scale=planes[:, g, BANK * b : BANK * (b + 1)],
                    start=(g == 0),
                    stop=(g == PASSES - 1),
                )
            return acc

        def cos_scalar(t, b, acc, t1c):
            view = acc[:].rearrange("p (h l e) -> p h l e", h=QH, l=IL)
            for l in range(IL):
                i = IL * b + l
                nc.scalar.activation(out=t1c[:, i, :, :], in_=view[:, :, l, :], func=COPY, scale=cosf[:, t, i : i + 1])

        def sin_vector(t, b, acc, t2q):
            nc.vector.tensor_tensor(
                out=t2q[:, :, IL * b : IL * (b + 1), :],
                in0=acc[:].rearrange("p (h l e) -> p h l e", h=QH, l=IL)[:, :, :, ::-1],
                in1=sin2[:, t, IL * b : IL * (b + 1), :].unsqueeze(1).to_broadcast([P, QH, IL, 2]),
                op=MULT,
            )

        def cos_k(t, acc, t1k):
            nc.vector.tensor_tensor(
                out=t1k[:],
                in0=acc[:].rearrange("p (h i e) -> p h i e", h=KH, e=2),
                in1=cosf[:, t, :].unsqueeze(1).unsqueeze(3).to_broadcast([P, KH, HALF, 2]),
                op=MULT,
            )

        def sin_k(t, acc, t2k):
            nc.vector.tensor_tensor(
                out=t2k[:],
                in0=acc[:].rearrange("p (h i e) -> p h i e", h=KH, e=2)[:, :, :, ::-1],
                in1=sin2[:, t, :, :].unsqueeze(1).to_broadcast([P, KH, HALF, 2]),
                op=MULT,
            )

        def add_k(engine, t, t1k, t2k):
            rok = work.tile([P, KH, HALF, 2], F32, name="rok")
            engine.tensor_tensor(out=rok[:], in0=t1k[:], in1=t2k[:], op=ADD)
            nc.sync.dma_start(out=k_out[P * t : P * (t + 1), :], in_=rok[:].rearrange("p h i e -> p (h i e)"))

        def cos_q3(t, acc, t1v):
            nc.vector.tensor_tensor(
                out=t1v[:],
                in0=acc[:].rearrange("p (h l e) -> p h l e", h=QH, l=IL),
                in1=cosf[:, t, SPAIRS:HALF].unsqueeze(1).unsqueeze(3).to_broadcast([P, QH, IL, 2]),
                op=MULT,
            )

        def add_bank(engine, b, t1c, t2q, roq):
            engine.tensor_tensor(
                out=roq[:, :, IL * b : IL * (b + 1), :],
                in0=t1c[:, IL * b : IL * (b + 1), :, :].rearrange("p i h e -> p h i e"),
                in1=t2q[:, :, IL * b : IL * (b + 1), :],
                op=ADD,
            )

        def add_q3(engine, t1v, t2q, roq):
            engine.tensor_tensor(
                out=roq[:, :, SPAIRS:HALF, :], in0=t1v[:], in1=t2q[:, :, SPAIRS:HALF, :], op=ADD
            )

        def add_heads(t1c, t2q, roq, h0, h1):
            nc.vector.tensor_tensor(
                out=roq[:, h0:h1, 0:SPAIRS, :],
                in0=t1c[:].rearrange("p i h e -> p h i e")[:, h0:h1, :, :],
                in1=t2q[:, h0:h1, 0:SPAIRS, :],
                op=ADD,
            )

        def store_q(t, roq, h0, h1):
            nc.sync.dma_start(
                out=q_out[P * t : P * (t + 1), P * h0 : P * h1],
                in_=roq[:, h0:h1, :, :].rearrange("p h i e -> p (h i e)"),
            )

        def project_tile(t):
            return [project(t, wq, wqs, b) for b in range(4)], project(t, ww, ws, 4), project(t, ww, ws, 5)

        def copy_k(t, acc_r):
            rok = work.tile([P, BANK], F32, name="rok")
            nc.scalar.copy(out=rok[:], in_=acc_r[:])
            nc.sync.dma_start(out=k_out[P * t : P * (t + 1), :], in_=rok[:])

        def finish(t, t1c, t2q, roq, t1k, t2k):
            add_bank(nc.vector, 2, t1c, t2q, roq)
            if t % 2 == 1:
                add_k(nc.vector, t, t1k, t2k)
            store_q(t, roq, 0, QH)

        acc_q, acc_k, acc_v = project_tile(0)
        waiting = None
        owed = None
        for t in range(TILES):
            last = t == TILES - 1
            t1c = work.tile([P, SPAIRS, QH, 2], F32, name="t1c")
            t1v = work.tile([P, QH, IL, 2], F32, name="t1v")
            t2q = work.tile([P, QH, HALF, 2], F32, name="t2q")
            roq = work.tile([P, QH, HALF, 2], F32, name="roq")
            t1k = work.tile([P, KH, HALF, 2], F32, name="t1k")
            t2k = work.tile([P, KH, HALF, 2], F32, name="t2k")
            vt = work.tile([P, BANK], F32, name="vt")
            for b in range(3):
                sin_vector(t, b, acc_q[b], t2q)
                cos_scalar(t, b, acc_q[b], t1c)
                if b == 1 and owed is not None:
                    finish(*owed)
                    owed = None
            if waiting is not None:
                copy_k(t - 1, waiting)
                waiting = None
            nc.scalar.copy(out=vt[:], in_=acc_v[:])
            if t == 0:
                nc.scalar.copy(out=cosf[:, 1:TILES, :], in_=cosb[:, 1:TILES, :])
            sin_vector(t, 3, acc_q[3], t2q)
            cos_q3(t, acc_q[3], t1v)
            cos_k(t, acc_k, t1k)
            sin_k(t, acc_k, t2k)
            if not last:
                acc_q, acc_k, acc_v = project_tile(t + 1)
            if t % 2 == 0:
                waiting = psum.tile([P, BANK], F32, name="acc")
                nc.tensor.matmul(out=waiting[:], lhsT=ident[:], rhs=t1k[:].rearrange("p h i e -> p (h i e)"), start=True, stop=False)
                nc.tensor.matmul(out=waiting[:], lhsT=ident[:], rhs=t2k[:].rearrange("p h i e -> p (h i e)"), start=False, stop=True)
            nc.sync.dma_start(out=v_out[P * t : P * (t + 1), :], in_=vt[:])
            if not last:
                add_bank(nc.gpsimd, 0, t1c, t2q, roq)
                add_bank(nc.gpsimd, 1, t1c, t2q, roq)
                add_q3(nc.gpsimd, t1v, t2q, roq)
                owed = (t, t1c, t2q, roq, t1k, t2k)
            else:
                add_q3(nc.vector, t1v, t2q, roq)
                add_k(nc.vector, t, t1k, t2k)
                for h0, h1 in ((0, 6), (6, 11), (11, 14), (14, QH)):
                    add_heads(t1c, t2q, roq, h0, h1)
                    store_q(t, roq, h0, h1)
